import numpy as np
import ml_dtypes


def mxq(x, axis, fmt="e4m3"):
    dtype, down = {"e4m3": (ml_dtypes.float8_e4m3fn, 7), "e5m2": (ml_dtypes.float8_e5m2, 14)}[fmt]
    v = np.moveaxis(np.asarray(x, np.float32).astype(ml_dtypes.bfloat16).astype(np.float64), axis, -1)
    blocks = v.reshape(v.shape[:-1] + (-1, 32))
    amax = np.abs(blocks).max(-1, keepdims=True)
    byte = np.maximum(np.where(amax > 0, np.frexp(amax)[1] - 1 + 127, 0) - down, 1)
    scale = np.exp2(byte - 127.0)
    codes = (blocks / scale).astype(np.float32).astype(dtype).astype(np.float64)
    return np.moveaxis((codes * scale).reshape(v.shape), -1, axis)


WIDE = False


def mx_kscale(k):
    if not WIDE:
        return np.ones(k)
    levels = np.array([10, -10, 5, -5, 0])
    a = np.random.permutation(np.resize(levels, k // 512 * 4)).reshape(k // 512, 4)
    idx = np.arange(k)
    return np.exp2(a[idx // 512, idx % 128 // 32])


BF16 = ml_dtypes.bfloat16


def bf(x):
    return np.asarray(x, np.float32).astype(BF16)


def f64(x):
    return np.asarray(x).astype(np.float64)


B, N, D, C, K, H = 2, 256, 128, 1024, 3072, 8


def _wn(W, g):
    return (g / np.sqrt(np.sum(W * W))) * W


def setup_inputs():
    s, t = mx_kscale(C), mx_kscale(K)
    Wv = bf(np.random.standard_normal((K, C)) * 0.5 / np.sqrt(C) / s * t[:, None])
    Wq = bf(np.random.standard_normal((K, C)) * 0.5 / np.sqrt(C) / s / t[:, None])
    gv = bf((2.0 + 0.2 * np.random.standard_normal(1)) * np.sqrt(np.sum(f64(Wv) ** 2)))
    gq = bf((2.0 + 0.2 * np.random.standard_normal(1)) * np.sqrt(np.sum(f64(Wq) ** 2)))
    return {"v": bf(np.random.standard_normal((B, N, C)) * s),
            "q": bf(np.random.standard_normal((B, D, C)) * s),
            "Wv": Wv,
            "gv": gv,
            "bv": bf(np.random.standard_normal(K) * 0.5 * t),
            "Wq": Wq,
            "gq": gq,
            "bq": bf(np.random.standard_normal(K) * 0.5 / t),
            "h_mat": bf(np.random.standard_normal((1, H, 1, K)) / np.sqrt(K)),
            "h_bias": bf(np.random.standard_normal((1, H, 1, 1)) * 0.5)}


def reference(v, q, Wv, gv, bv, Wq, gq, bq, h_mat, h_bias):
    wv = _wn(f64(Wv), f64(gv))
    wq = _wn(f64(Wq), f64(gq))
    v_ = (mxq(f64(v), 2, "e4m3") @ mxq(wv, 1, "e4m3").T) + f64(bv)
    q_ = (mxq(f64(q), 2, "e4m3") @ mxq(wq, 1, "e4m3").T) + f64(bq)
    hm = f64(h_mat)[0, :, 0, :]
    hv = hm[None, :, None, :] * v_[:, None, :, :]
    logits = (mxq(hv, 3, "e4m3") @ mxq(q_, 2, "e4m3")[:, None, :, :].transpose(0, 1, 3, 2)) + f64(h_bias)
    return logits

@@ -1,0 +1,345 @@
+from contextlib import ExitStack
+
+import concourse.mybir as mybir
+from concourse.masks import make_identity
+
+F32 = mybir.dt.float32
+BF16 = mybir.dt.bfloat16
+U32 = mybir.dt.uint32
+U8 = mybir.dt.uint8
+I32 = mybir.dt.int32
+FP8X4 = mybir.dt.float8_e4m3fn_x4
+ACT = mybir.ActivationFunctionType
+ALU = mybir.AluOpType
+AX = mybir.AxisListType
+
+P = 128
+B, N, D, C, K, H = 2, 256, 128, 1024, 3072, 8
+G = K // 512
+FLOPS = 2 * (B * N * K * C + B * D * K * C + B * H * N * D * K)
+
+GRAM_BLOCKS = 15
+EVAC_S = {"q": 0, "v": 3}
+VPATH = ((0,), (0,), (0,), (0,), (0,), (0,), (0,), (0,))
+
+
+def tile_bcnet_kernel(tc, v, q, Wv, gv, bv, Wq, gq, bq, h_mat, h_bias, out):
+    nc = tc.nc
+    with ExitStack() as ctx:
+        const = ctx.enter_context(tc.tile_pool(name="const", bufs=1))
+        natp = ctx.enter_context(tc.tile_pool(name="natp", bufs=4))
+        grpp = ctx.enter_context(tc.tile_pool(name="grpp", bufs=9))
+        codp = ctx.enter_context(tc.tile_pool(name="codp", bufs=3))
+        hcp = ctx.enter_context(tc.tile_pool(name="hcp", bufs=2))
+        outp = ctx.enter_context(tc.tile_pool(name="outp", bufs=2))
+        ps_t = ctx.enter_context(tc.psum_pool(name="ps_t", bufs=3))
+        ps_m = ctx.enter_context(tc.psum_pool(name="ps_m", bufs=3))
+        ps_a = ctx.enter_context(tc.psum_pool(name="ps_a", bufs=2))
+
+        warm = const.tile([P, 1], F32, name="warm")
+        nc.vector.memset(warm[:], 1.0)
+        warm2 = const.tile([P, 1], F32, name="warm2")
+        nc.scalar.activation(out=warm2[:], in_=warm[:], func=ACT.Sqrt)
+
+        xrows = natp.tile([P, K], BF16, tag="nat", name="xrows")
+        nc.vector.memset(xrows[:].bitcast(I32), 0)
+        nc.scalar.dma_start(out=xrows[0:1, :], in_=bv.rearrange("(o k) -> o k", o=1))
+        nc.scalar.dma_start(out=xrows[1:2, :], in_=bq.rearrange("(o k) -> o k", o=1))
+        nc.scalar.dma_start(out=xrows[2:10, :], in_=h_mat.rearrange("a h b k -> (a h b) k"))
+        g_b = {}
+        for w, g_in in (("q", gq), ("v", gv)):
+            g_b[w] = const.tile([P, 1], BF16, name="g_b_" + w)
+            nc.scalar.dma_start(out=g_b[w][:], in_=g_in.partition_broadcast(P))
+        hb_b = const.tile([P, H], BF16, name="hb_b")
+        nc.scalar.dma_start(out=hb_b[:], in_=h_bias.rearrange("a h b c -> (a h b c)").partition_broadcast(P))
+        hb = const.tile([P, H], F32, name="hb")
+        nc.vector.tensor_copy(out=hb[:], in_=hb_b[:])
+
+        ident_f = const.tile([P, P], F32, name="ident_f")
+        make_identity(nc, ident_f[:])
+        ident_b = const.tile([P, P], BF16, name="ident_b")
+        make_identity(nc, ident_b[:])
+        ones_f = const.tile([P, P], F32, name="ones_f")
+        nc.vector.memset(ones_f[:], 1.0)
+
+        accs = {}
+        for w in ("q", "v"):
+            accs[w] = const.tile([P, P + 8], F32, name="accs_" + w)
+            nc.vector.memset(accs[w][:], 0.0)
+        junk = const.tile([P, 4096 - P * GRAM_BLOCKS], BF16, name="junk")
+
+        qnat = natp.tile([P, B, C], BF16, tag="nat", name="qnat")
+        nc.sync.dma_start(out=qnat[:], in_=q.rearrange("b p c -> p b c"))
+
+        sm = const.tile([P, 4 * G, 10], F32, name="sm")
+        xv = xrows[:].rearrange("p (g m t) -> p g t m", g=G, t=4)
+        for a in range(3):
+            tps = ps_t.tile([P, 8, P], BF16, tag="tp", name="tps")
+            for i in range(8):
+                gt = 8 * a + i
+                nc.tensor.transpose(tps[:, i, :], xv[:, gt // 4, gt % 4, :], ident_b[:])
+            nc.vector.tensor_copy(out=sm[:, 8 * a : 8 * a + 8, :], in_=tps[:, :, 0:10])
+
+        copy_engines = {"s": nc.scalar.copy, "v": nc.vector.tensor_copy}
+
+        def prepare_x(tiles, name):
+            cols = P * len(tiles)
+            xg = grpp.tile([P, 2, cols, 4], BF16, tag="grp", name=name + "g", align_bytes=64)
+            xgw = xg[:].rearrange("p a m e -> p (a m e)").bitcast(F32).rearrange("p (a m u) -> p a m u", a=2, u=2)
+            n = 0
+            for a in range(2):
+                for pr in range(len(tiles) // 2):
+                    bank = ps_t.tile([P, 2, 2, P], F32, tag="tp", name="bank")
+                    for u in range(2):
+                        for i in range(2):
+                            j = 2 * a + u
+                            nc.tensor.transpose(bank[:, u, i, :], tiles[2 * pr + i][:, P * j : P * j + P], ident_f[:])
+                    copy_engines["sv"[n % 2]](
+                        out=xgw[:, a, 256 * pr : 256 * pr + 256, :], in_=bank[:].rearrange("p u i m -> p (i m) u")
+                    )
+                    n += 1
+            xc = const.tile([P, 2, cols], U32, name=name + "c", align_bytes=64)
+            xs = const.tile([P, 2, cols], U8, name=name + "s", align_bytes=64)
+            nc.vector.quantize_mx(
+                out=xc[:].rearrange("p a m -> p (a m)").bitcast(FP8X4),
+                scales=xs[:].rearrange("p a m -> p (a m)"),
+                in_=xg[:].rearrange("p a m e -> p (a m e)"),
+            )
+            return xc, xs
+
+        qw = qnat[:].rearrange("p b c -> p (b c)").bitcast(F32)
+        qxc, qxs = prepare_x([qw[:, 512 * i : 512 * i + 512] for i in range(2)], "qx")
+
+        gram = {}
+
+        def pre_norm(w, W, g):
+            if g == 0:
+                gram[w] = ps_m.tile([P, 512], F32, tag="misc", name="gram")
+            nat = natp.tile([P, 4 * C], BF16, tag="nat", name="nat")
+            nc.sync.dma_start(out=nat[:], in_=W[512 * g : 512 * g + 512, :].rearrange("(p t) c -> p (t c)", t=4))
+            for i in range(GRAM_BLOCKS):
+                blk = nat[:, P * i : P * i + P]
+                nc.tensor.matmul(
+                    gram[w][:, 0:P],
+                    lhsT=blk,
+                    rhs=blk,
+                    start=(g == 0 and i == 0),
+                    stop=(g == G - 1 and i == GRAM_BLOCKS - 1),
+                )
+            nc.scalar.activation(
+                out=junk[:],
+                in_=nat[:, P * GRAM_BLOCKS :],
+                func=ACT.Square,
+                accum_out=accs[w][:, P + g : P + g + 1],
+            )
+            natw = nat[:].bitcast(F32)
+            grp = grpp.tile([P, 2, 512, 4], BF16, tag="grp", name="grp", align_bytes=64)
+            grpw = grp[:].rearrange("p a m e -> p (a m e)").bitcast(F32).rearrange("p (a m u) -> p a m u", a=2, u=2)
+            n = 0
+            for a in range(2):
+                for hf in range(2):
+                    bank = ps_t.tile([P, 2, 2, P], F32, tag="tp", name="bank")
+                    for u in range(2):
+                        for i in range(2):
+                            t = 2 * hf + i
+                            j = 2 * a + u
+                            nc.tensor.transpose(
+                                bank[:, u, i, :], natw[:, 512 * t + P * j : 512 * t + P * j + P], ident_f[:]
+                            )
+                    copy_engines["s" if n < EVAC_S[w] else "v"](
+                        out=grpw[:, a, 256 * hf : 256 * hf + 256, :], in_=bank[:].rearrange("p u i m -> p (i m) u")
+                    )
+                    n += 1
+            return grp
+
+        def norm_chain(w):
+            nc.vector.tensor_tensor(out=accs[w][:, 0:P], in0=gram[w][:, 0:P], in1=ident_f[:], op=ALU.mult)
+            tot_ps = ps_m.tile([P, 512], F32, tag="misc", name="tot_ps")
+            nc.tensor.matmul(tot_ps[:, 0 : P + 8], lhsT=ones_f[:], rhs=accs[w][:], start=True, stop=True)
+            tot = const.tile([P, 1], F32, name="tot_" + w)
+            nc.vector.reduce_sum(out=tot[:], in_=tot_ps[:, 0 : P + 8], axis=AX.X)
+            root = const.tile([P, 1], F32, name="root_" + w)
+            nc.scalar.activation(out=root[:], in_=tot[:], func=ACT.Sqrt)
+            inv = const.tile([P, 1], F32, name="inv_" + w)
+            nc.vector.reciprocal(out=inv[:], in_=root[:])
+            s = const.tile([P, 1], F32, name="s_" + w)
+            nc.vector.tensor_tensor(out=s[:], in0=inv[:], in1=g_b[w][:], op=ALU.mult)
+            return s
+
+        def scale_chunk(grp, s):
+            flat = grp[:].rearrange("p a m e -> p (a m e)")
+            nc.vector.tensor_scalar(out=flat, in0=flat, scalar1=s[:, 0:1], scalar2=None, op0=ALU.mult)
+
+        def quantise_chunk(grp):
+            wc = codp.tile([P, 2, 512], U32, tag="wc", name="wc", align_bytes=64)
+            ws = codp.tile([P, 2, 512], U8, tag="ws", name="ws", align_bytes=64)
+            nc.vector.quantize_mx(
+                out=wc[:].rearrange("p a m -> p (a m)").bitcast(FP8X4),
+                scales=ws[:].rearrange("p a m -> p (a m)"),
+                in_=grp[:].rearrange("p a m e -> p (a m e)"),
+            )
+            return wc, ws
+
+        grps_q = [pre_norm("q", Wq, g) for g in range(G)]
+        vnat = natp.tile([P, B, 2 * C], BF16, tag="nat", name="vnat")
+        nc.sync.dma_start(out=vnat[:], in_=v.rearrange("b (p r) c -> p b (r c)", r=2))
+        s_q = norm_chain("q")
+
+        vw = vnat[:].rearrange("p b c -> p (b c)").bitcast(F32)
+        vxc, vxs = prepare_x([vw[:, 512 * i : 512 * i + 512] for i in range(4)], "vx")
+
+        qc = const.tile([P, G, B * D], U32, name="qc", align_bytes=64)
+        qs = const.tile([P, G, B * D], U8, name="qs", align_bytes=64)
+        q_banks = {}
+        q_grouped = {}
+
+        def q_project(g):
+            wc, ws = quantise_chunk(grps_q[g])
+            q_banks[g] = []
+            for b in range(B):
+                bank = ps_a.tile([P, 4, D], F32, tag="acc", name="qbank")
+                for t in range(4):
+                    for a in range(2):
+                        nc.tensor.matmul_mx(
+                            out=bank[:, t, :],
+                            lhsT=wc[:, a, P * t : P * t + P].bitcast(FP8X4),
+                            lhsT_scale=ws[:, a, P * t : P * t + P],
+                            rhs=qxc[:, a, D * b : D * b + D].bitcast(FP8X4),
+                            rhs_scale=qxs[:, a, D * b : D * b + D],
+                            start=(a == 0),
+                            stop=(a == 1),
+                        )
+                q_banks[g].append(bank)
+
+        def q_bias(g):
+            qg = codp.tile([P, B, D, 4], BF16, tag="qg", name="qg", align_bytes=64, bufs=2)
+            for b in range(B):
+                nc.vector.tensor_tensor(
+                    out=qg[:, b, :, :],
+                    in0=q_banks[g][b][:].rearrange("p t d -> p d t"),
+                    in1=sm[:, 4 * g : 4 * g + 4, 1].unsqueeze(1).to_broadcast([P, D, 4]),
+                    op=ALU.add,
+                )
+            q_grouped[g] = qg
+
+        def q_quantise(g):
+            nc.vector.quantize_mx(
+                out=qc[:, g, :].bitcast(FP8X4),
+                scales=qs[:, g, :],
+                in_=q_grouped[g][:].rearrange("p b d t -> p (b d t)"),
+            )
+
+        grps_v = []
+        for i in range(G + 3):
+            if i < G:
+                grps_v.append(pre_norm("v", Wv, i))
+                scale_chunk(grps_q[i], s_q)
+            if 0 <= i - 3 < G:
+                q_quantise(i - 3)
+            if 0 <= i - 2 < G:
+                q_bias(i - 2)
+            if 0 <= i - 1 < G:
+                q_project(i - 1)
+        s_v = norm_chain("v")
+
+        v_sb = const.tile([P, G, 4, B * N], F32, name="v_sb")
+
+        def v_project(g):
+            wc, ws = quantise_chunk(grps_v[g])
+            for t in range(4):
+                bank = ps_a.tile([P, B * N], F32, tag="acc", name="vbank")
+                for a in range(2):
+                    nc.tensor.matmul_mx(
+                        out=bank[:],
+                        lhsT=wc[:, a, P * t : P * t + P].bitcast(FP8X4),
+                        lhsT_scale=ws[:, a, P * t : P * t + P],
+                        rhs=vxc[:, a, :].bitcast(FP8X4),
+                        rhs_scale=vxs[:, a, :],
+                        start=(a == 0),
+                        stop=(a == 1),
+                    )
+                nc.scalar.activation(
+                    out=v_sb[:, g, t, :], in_=bank[:], func=ACT.Identity, bias=sm[:, 4 * g + t, 0:1], scale=1.0
+                )
+
+        for i in range(G + 1):
+            if i < G:
+                scale_chunk(grps_v[i], s_v)
+            if i >= 1:
+                v_project(i - 1)
+
+        head_codes = {}
+        pair_tiles = {}
+
+        def hv_unit(h, gp, j):
+            g = 2 * gp + j
+            hg, hp = pair_tiles[(h, gp)]
+            if g in VPATH[h]:
+                nc.vector.tensor_tensor(
+                    out=hg[:, j, :, :],
+                    in0=v_sb[:, g, :, :].rearrange("p t n -> p n t"),
+                    in1=sm[:, 4 * g : 4 * g + 4, 2 + h].unsqueeze(1).to_broadcast([P, B * N, 4]),
+                    op=ALU.mult,
+                )
+            else:
+                for t in range(4):
+                    nc.scalar.activation(
+                        out=hp[:, j, t, :],
+                        in_=v_sb[:, g, t, :],
+                        func=ACT.Copy,
+                        scale=sm[:, 4 * g + t, 2 + h : 3 + h],
+                    )
+                nc.vector.tensor_copy(
+                    out=hg[:, j, :, :].rearrange("p (c i) t -> p c t i", i=4),
+                    in_=hp[:, j, :, :].rearrange("p t (c i) -> p c t i", i=4),
+                )
+
+        def hv_quantise(h, gp):
+            hc, hs = head_codes[h]
+            hg = pair_tiles[(h, gp)][0]
+            nc.vector.quantize_mx(
+                out=hc[:, 2 * gp : 2 * gp + 2, :].rearrange("p g n -> p (g n)").bitcast(FP8X4),
+                scales=hs[:, 2 * gp : 2 * gp + 2, :].rearrange("p g n -> p (g n)"),
+                in_=hg[:].rearrange("p j n t -> p (j n t)"),
+            )
+
+        def logits(h):
+            hc, hs = head_codes[h]
+            lg = ps_m.tile([P, 4, D], F32, tag="misc", name="lg")
+            for br in range(4):
+                b = br // 2
+                for g in range(G):
+                    nc.tensor.matmul_mx(
+                        out=lg[:, br, :],
+                        lhsT=hc[:, g, P * br : P * br + P].bitcast(FP8X4),
+                        lhsT_scale=hs[:, g, P * br : P * br + P],
+                        rhs=qc[:, g, D * b : D * b + D].bitcast(FP8X4),
+                        rhs_scale=qs[:, g, D * b : D * b + D],
+                        start=(g == 0),
+                        stop=(g == G - 1),
+                    )
+            o_sb = outp.tile([P, 4, D], F32, tag="o", name="o_sb")
+            nc.scalar.activation(out=o_sb[:], in_=lg[:], func=ACT.Identity, bias=hb[:, h : h + 1], scale=1.0)
+            nc.sync.dma_start(
+                out=out[:, h].rearrange("b (m r) d -> m b (r d)", r=2),
+                in_=o_sb[:].rearrange("p (b r) d -> p b (r d)", b=2),
+            )
+
+        pairs = [(h, gp) for h in range(H) for gp in range(G // 2)]
+        for i in range(len(pairs) + 1):
+            if i < len(pairs):
+                h, gp = pairs[i]
+                if gp == 0:
+                    hc_t = hcp.tile([P, G, B * N], U32, tag="hc", name="hc_t", align_bytes=64)
+                    hs_t = hcp.tile([P, G, B * N], U8, tag="hs", name="hs_t", align_bytes=64)
+                    head_codes[h] = (hc_t, hs_t)
+                hg_t = grpp.tile([P, 2, B * N, 4], BF16, tag="grp", name="hg_t", align_bytes=64)
+                hp_t = natp.tile([P, 2, 4, B * N], BF16, tag="nat", name="hp_t")
+                pair_tiles[(h, gp)] = (hg_t, hp_t)
+                hv_unit(h, gp, 0)
+            if i >= 1:
+                hv_quantise(pairs[i - 1][0], pairs[i - 1][1])
+                if pairs[i - 1][1] == G // 2 - 1:
+                    logits(pairs[i - 1][0])
+            if i < len(pairs):
+                hv_unit(pairs[i][0], pairs[i][1], 1)

@@ -19,7 +19,7 @@ G = K // 512
 FLOPS = 2 * (B * N * K * C + B * D * K * C + B * H * N * D * K)
 
 GRAM_BLOCKS = 15
-EVAC_S = {"q": 0, "v": 3}
+EVAC_S = {"q": 3, "v": 0}
 VPATH = ((0,), (0,), (0,), (0,), (0,), (0,), (0,), (0,))
 
 
@@ -27,7 +27,8 @@ def tile_bcnet_kernel(tc, v, q, Wv, gv, bv, Wq, gq, bq, h_mat, h_bias, out):
     nc = tc.nc
     with ExitStack() as ctx:
         const = ctx.enter_context(tc.tile_pool(name="const", bufs=1))
-        natp = ctx.enter_context(tc.tile_pool(name="natp", bufs=4))
+        natp = ctx.enter_context(tc.tile_pool(name="natp", bufs=3))
+        hpp = ctx.enter_context(tc.tile_pool(name="hpp", bufs=3))
         grpp = ctx.enter_context(tc.tile_pool(name="grpp", bufs=9))
         codp = ctx.enter_context(tc.tile_pool(name="codp", bufs=3))
         hcp = ctx.enter_context(tc.tile_pool(name="hcp", bufs=2))
@@ -41,7 +42,7 @@ def tile_bcnet_kernel(tc, v, q, Wv, gv, bv, Wq, gq, bq, h_mat, h_bias, out):
         warm2 = const.tile([P, 1], F32, name="warm2")
         nc.scalar.activation(out=warm2[:], in_=warm[:], func=ACT.Sqrt)
 
-        xrows = natp.tile([P, K], BF16, tag="nat", name="xrows")
+        xrows = grpp.tile([P, K], BF16, tag="grp", name="xrows", align_bytes=64)
         nc.vector.memset(xrows[:].bitcast(I32), 0)
         nc.scalar.dma_start(out=xrows[0:1, :], in_=bv.rearrange("(o k) -> o k", o=1))
         nc.scalar.dma_start(out=xrows[1:2, :], in_=bq.rearrange("(o k) -> o k", o=1))
@@ -68,8 +69,8 @@ def tile_bcnet_kernel(tc, v, q, Wv, gv, bv, Wq, gq, bq, h_mat, h_bias, out):
             nc.vector.memset(accs[w][:], 0.0)
         junk = const.tile([P, 4096 - P * GRAM_BLOCKS], BF16, name="junk")
 
-        qnat = natp.tile([P, B, C], BF16, tag="nat", name="qnat")
-        nc.sync.dma_start(out=qnat[:], in_=q.rearrange("b p c -> p b c"))
+        vnat = natp.tile([P, B, 2 * C], BF16, tag="nat", name="vnat")
+        nc.sync.dma_start(out=vnat[:], in_=v.rearrange("b (p r) c -> p b (r c)", r=2))
 
         sm = const.tile([P, 4 * G, 10], F32, name="sm")
         xv = xrows[:].rearrange("p (g m t) -> p g t m", g=G, t=4)
@@ -107,8 +108,8 @@ def tile_bcnet_kernel(tc, v, q, Wv, gv, bv, Wq, gq, bq, h_mat, h_bias, out):
             )
             return xc, xs
 
-        qw = qnat[:].rearrange("p b c -> p (b c)").bitcast(F32)
-        qxc, qxs = prepare_x([qw[:, 512 * i : 512 * i + 512] for i in range(2)], "qx")
+        vw = vnat[:].rearrange("p b c -> p (b c)").bitcast(F32)
+        vxc, vxs = prepare_x([vw[:, 512 * i : 512 * i + 512] for i in range(4)], "vx")
 
         gram = {}
 
@@ -180,13 +181,41 @@ def tile_bcnet_kernel(tc, v, q, Wv, gv, bv, Wq, gq, bq, h_mat, h_bias, out):
             )
             return wc, ws
 
-        grps_q = [pre_norm("q", Wq, g) for g in range(G)]
-        vnat = natp.tile([P, B, 2 * C], BF16, tag="nat", name="vnat")
-        nc.sync.dma_start(out=vnat[:], in_=v.rearrange("b (p r) c -> p b (r c)", r=2))
-        s_q = norm_chain("q")
+        grps_v = [pre_norm("v", Wv, g) for g in range(G)]
+        s_v = norm_chain("v")
+        qnat = natp.tile([P, B, C], BF16, tag="nat", name="qnat")
+        nc.sync.dma_start(out=qnat[:], in_=q.rearrange("b p c -> p b c"))
 
-        vw = vnat[:].rearrange("p b c -> p (b c)").bitcast(F32)
-        vxc, vxs = prepare_x([vw[:, 512 * i : 512 * i + 512] for i in range(4)], "vx")
+        v_sb = const.tile([P, G, 4, B * N], F32, name="v_sb")
+
+        def v_project(g):
+            wc, ws = quantise_chunk(grps_v[g])
+            for t in range(4):
+                bank = ps_a.tile([P, B * N], F32, tag="acc", name="vbank")
+                for a in range(2):
+                    nc.tensor.matmul_mx(
+                        out=bank[:],
+                        lhsT=wc[:, a, P * t : P * t + P].bitcast(FP8X4),
+                        lhsT_scale=ws[:, a, P * t : P * t + P],
+                        rhs=vxc[:, a, :].bitcast(FP8X4),
+                        rhs_scale=vxs[:, a, :],
+                        start=(a == 0),
+                        stop=(a == 1),
+                    )
+                nc.scalar.activation(
+                    out=v_sb[:, g, t, :], in_=bank[:], func=ACT.Identity, bias=sm[:, 4 * g + t, 0:1], scale=1.0
+                )
+
+        for i in range(G + 1):
+            if i < G:
+                scale_chunk(grps_v[i], s_v)
+            if i >= 1:
+                v_project(i - 1)
+
+        qw = qnat[:].rearrange("p b c -> p (b c)").bitcast(F32)
+        qxc, qxs = prepare_x([qw[:, 512 * i : 512 * i + 512] for i in range(2)], "qx")
+        grps_q = [pre_norm("q", Wq, g) for g in range(G)]
+        s_q = norm_chain("q")
 
         qc = const.tile([P, G, B * D], U32, name="qc", align_bytes=64)
         qs = const.tile([P, G, B * D], U8, name="qs", align_bytes=64)
@@ -229,10 +258,8 @@ def tile_bcnet_kernel(tc, v, q, Wv, gv, bv, Wq, gq, bq, h_mat, h_bias, out):
                 in_=q_grouped[g][:].rearrange("p b d t -> p (b d t)"),
             )
 
-        grps_v = []
         for i in range(G + 3):
             if i < G:
-                grps_v.append(pre_norm("v", Wv, i))
                 scale_chunk(grps_q[i], s_q)
             if 0 <= i - 3 < G:
                 q_quantise(i - 3)
@@ -240,40 +267,13 @@ def tile_bcnet_kernel(tc, v, q, Wv, gv, bv, Wq, gq, bq, h_mat, h_bias, out):
                 q_bias(i - 2)
             if 0 <= i - 1 < G:
                 q_project(i - 1)
-        s_v = norm_chain("v")
-
-        v_sb = const.tile([P, G, 4, B * N], F32, name="v_sb")
-
-        def v_project(g):
-            wc, ws = quantise_chunk(grps_v[g])
-            for t in range(4):
-                bank = ps_a.tile([P, B * N], F32, tag="acc", name="vbank")
-                for a in range(2):
-                    nc.tensor.matmul_mx(
-                        out=bank[:],
-                        lhsT=wc[:, a, P * t : P * t + P].bitcast(FP8X4),
-                        lhsT_scale=ws[:, a, P * t : P * t + P],
-                        rhs=vxc[:, a, :].bitcast(FP8X4),
-                        rhs_scale=vxs[:, a, :],
-                        start=(a == 0),
-                        stop=(a == 1),
-                    )
-                nc.scalar.activation(
-                    out=v_sb[:, g, t, :], in_=bank[:], func=ACT.Identity, bias=sm[:, 4 * g + t, 0:1], scale=1.0
-                )
-
-        for i in range(G + 1):
-            if i < G:
-                scale_chunk(grps_v[i], s_v)
-            if i >= 1:
-                v_project(i - 1)
 
         head_codes = {}
         pair_tiles = {}
 
         def hv_unit(h, gp, j):
             g = 2 * gp + j
-            hg, hp = pair_tiles[(h, gp)]
+            hg = pair_tiles[(h, gp)]
             if g in VPATH[h]:
                 nc.vector.tensor_tensor(
                     out=hg[:, j, :, :],
@@ -282,21 +282,22 @@ def tile_bcnet_kernel(tc, v, q, Wv, gv, bv, Wq, gq, bq, h_mat, h_bias, out):
                     op=ALU.mult,
                 )
             else:
+                hp = hpp.tile([P, 4, B * N], BF16, tag="hp", name="hp")
                 for t in range(4):
                     nc.scalar.activation(
-                        out=hp[:, j, t, :],
+                        out=hp[:, t, :],
                         in_=v_sb[:, g, t, :],
                         func=ACT.Copy,
                         scale=sm[:, 4 * g + t, 2 + h : 3 + h],
                     )
                 nc.vector.tensor_copy(
                     out=hg[:, j, :, :].rearrange("p (c i) t -> p c t i", i=4),
-                    in_=hp[:, j, :, :].rearrange("p t (c i) -> p c t i", i=4),
+                    in_=hp[:].rearrange("p t (c i) -> p c t i", i=4),
                 )
 
         def hv_quantise(h, gp):
             hc, hs = head_codes[h]
-            hg = pair_tiles[(h, gp)][0]
+            hg = pair_tiles[(h, gp)]
             nc.vector.quantize_mx(
                 out=hc[:, 2 * gp : 2 * gp + 2, :].rearrange("p g n -> p (g n)").bitcast(FP8X4),
                 scales=hs[:, 2 * gp : 2 * gp + 2, :].rearrange("p g n -> p (g n)"),
@@ -334,8 +335,7 @@ def tile_bcnet_kernel(tc, v, q, Wv, gv, bv, Wq, gq, bq, h_mat, h_bias, out):
                     hs_t = hcp.tile([P, G, B * N], U8, tag="hs", name="hs_t", align_bytes=64)
                     head_codes[h] = (hc_t, hs_t)
                 hg_t = grpp.tile([P, 2, B * N, 4], BF16, tag="grp", name="hg_t", align_bytes=64)
-                hp_t = natp.tile([P, 2, 4, B * N], BF16, tag="nat", name="hp_t")
-                pair_tiles[(h, gp)] = (hg_t, hp_t)
+                pair_tiles[(h, gp)] = hg_t
                 hv_unit(h, gp, 0)
             if i >= 1:
                 hv_quantise(pairs[i - 1][0], pairs[i - 1][1])

@@ -7,7 +7,6 @@ F32 = mybir.dt.float32
 BF16 = mybir.dt.bfloat16
 U32 = mybir.dt.uint32
 U8 = mybir.dt.uint8
-I32 = mybir.dt.int32
 FP8X4 = mybir.dt.float8_e4m3fn_x4
 ACT = mybir.ActivationFunctionType
 ALU = mybir.AluOpType
@@ -19,107 +18,128 @@ G = K // 512
 FLOPS = 2 * (B * N * K * C + B * D * K * C + B * H * N * D * K)
 
 GRAM_BLOCKS = 15
-EVAC_S = {"q": 3, "v": 0}
-VPATH = ((0,), (0,), (0,), (0,), (0,), (0,), (0,), (0,))
+NAT_BUFS = 4
+X_AT = 3
+SMALL_AT = 4
+EVAC = {"q": "vvvv", "v": "sssv"}
+VPATH = ((2, 5), (0,), (0,), (0,), (0,), (0,), (0,), (0,))
+S_AHEAD = 2
+EVAC_LAG = 4
 
 
 def tile_bcnet_kernel(tc, v, q, Wv, gv, bv, Wq, gq, bq, h_mat, h_bias, out):
     nc = tc.nc
     with ExitStack() as ctx:
         const = ctx.enter_context(tc.tile_pool(name="const", bufs=1))
-        natp = ctx.enter_context(tc.tile_pool(name="natp", bufs=3))
-        hpp = ctx.enter_context(tc.tile_pool(name="hpp", bufs=3))
-        grpp = ctx.enter_context(tc.tile_pool(name="grpp", bufs=9))
+        natp = ctx.enter_context(tc.tile_pool(name="natp", bufs=NAT_BUFS))
+        hpp = ctx.enter_context(tc.tile_pool(name="hpp", bufs=S_AHEAD + 1))
+        grpp = ctx.enter_context(tc.tile_pool(name="grpp", bufs=8))
         codp = ctx.enter_context(tc.tile_pool(name="codp", bufs=3))
         hcp = ctx.enter_context(tc.tile_pool(name="hcp", bufs=2))
         outp = ctx.enter_context(tc.tile_pool(name="outp", bufs=2))
         ps_t = ctx.enter_context(tc.psum_pool(name="ps_t", bufs=3))
         ps_m = ctx.enter_context(tc.psum_pool(name="ps_m", bufs=3))
         ps_a = ctx.enter_context(tc.psum_pool(name="ps_a", bufs=2))
+        ctx.enter_context(tc.manual_schedule())
+
+        W_in = {"q": Wq, "v": Wv}
+        nat = {}
+        grp = {}
+        banks = {}
+        gram = {}
+        codes = {}
+
+        loads = [("q", g) for g in range(G)] + [("x", "v")] + [("v", g) for g in range(G)]
+        loads = loads[:X_AT] + [("x", "q")] + loads[X_AT:]
+        issued = [0]
+
+        late = {}
+
+        def next_load():
+            if issued[0] == len(loads):
+                if not late:
+                    late["bv"] = spread("bv", bv.rearrange("(g p t) -> p g t", p=P, t=4), 1, nc.sync)
+                    late["hm"] = spread("hm", h_mat.rearrange("a h b (g p t) -> p (a h b g) t", p=P, t=4), H, nc.sync)
+                return
+            w, g = loads[issued[0]]
+            issued[0] += 1
+            if w == "x":
+                src = q.rearrange("b p c -> p b c") if g == "q" else v.rearrange("b (p r) c -> p b (r c)", r=2)
+                nat[(w, g)] = natp.tile([P, B, src.shape[2]], BF16, tag="nat", name="xnat")
+                nc.sync.dma_start(out=nat[(w, g)][:], in_=src)
+            else:
+                nat[(w, g)] = natp.tile([P, 4 * C], BF16, tag="nat", name="nat")
+                nc.sync.dma_start(
+                    out=nat[(w, g)][:], in_=W_in[w][512 * g : 512 * g + 512, :].rearrange("(p t) c -> p (t c)", t=4)
+                )
+
+        for g in range(NAT_BUFS):
+            next_load()
 
         warm = const.tile([P, 1], F32, name="warm")
         nc.vector.memset(warm[:], 1.0)
         warm2 = const.tile([P, 1], F32, name="warm2")
         nc.scalar.activation(out=warm2[:], in_=warm[:], func=ACT.Sqrt)
 
-        xrows = grpp.tile([P, K], BF16, tag="grp", name="xrows", align_bytes=64)
-        nc.vector.memset(xrows[:].bitcast(I32), 0)
-        nc.scalar.dma_start(out=xrows[0:1, :], in_=bv.rearrange("(o k) -> o k", o=1))
-        nc.scalar.dma_start(out=xrows[1:2, :], in_=bq.rearrange("(o k) -> o k", o=1))
-        nc.scalar.dma_start(out=xrows[2:10, :], in_=h_mat.rearrange("a h b k -> (a h b) k"))
+        def spread(name, src, rows, queue):
+            raw = const.tile([P, rows * 4 * G], BF16, name=name + "_b")
+            queue.dma_start(out=raw[:].rearrange("p (r t) -> p r t", t=4), in_=src)
+            return raw
+
+        def widen(name, raw):
+            wide = const.tile([P, raw.shape[1]], F32, name=name)
+            nc.vector.tensor_copy(out=wide[:], in_=raw[:])
+            return wide
+
+        bq_b = spread("bq", bq.rearrange("(g p t) -> p g t", p=P, t=4), 1, nc.scalar)
         g_b = {}
         for w, g_in in (("q", gq), ("v", gv)):
             g_b[w] = const.tile([P, 1], BF16, name="g_b_" + w)
             nc.scalar.dma_start(out=g_b[w][:], in_=g_in.partition_broadcast(P))
         hb_b = const.tile([P, H], BF16, name="hb_b")
         nc.scalar.dma_start(out=hb_b[:], in_=h_bias.rearrange("a h b c -> (a h b c)").partition_broadcast(P))
-        hb = const.tile([P, H], F32, name="hb")
-        nc.vector.tensor_copy(out=hb[:], in_=hb_b[:])
 
         ident_f = const.tile([P, P], F32, name="ident_f")
         make_identity(nc, ident_f[:])
-        ident_b = const.tile([P, P], BF16, name="ident_b")
-        make_identity(nc, ident_b[:])
         ones_f = const.tile([P, P], F32, name="ones_f")
         nc.vector.memset(ones_f[:], 1.0)
-
         accs = {}
         for w in ("q", "v"):
             accs[w] = const.tile([P, P + 8], F32, name="accs_" + w)
             nc.vector.memset(accs[w][:], 0.0)
         junk = const.tile([P, 4096 - P * GRAM_BLOCKS], BF16, name="junk")
 
-        vnat = natp.tile([P, B, 2 * C], BF16, tag="nat", name="vnat")
-        nc.sync.dma_start(out=vnat[:], in_=v.rearrange("b (p r) c -> p b (r c)", r=2))
-
-        sm = const.tile([P, 4 * G, 10], F32, name="sm")
-        xv = xrows[:].rearrange("p (g m t) -> p g t m", g=G, t=4)
-        for a in range(3):
-            tps = ps_t.tile([P, 8, P], BF16, tag="tp", name="tps")
-            for i in range(8):
-                gt = 8 * a + i
-                nc.tensor.transpose(tps[:, i, :], xv[:, gt // 4, gt % 4, :], ident_b[:])
-            nc.vector.tensor_copy(out=sm[:, 8 * a : 8 * a + 8, :], in_=tps[:, :, 0:10])
-
         copy_engines = {"s": nc.scalar.copy, "v": nc.vector.tensor_copy}
 
-        def prepare_x(tiles, name):
-            cols = P * len(tiles)
-            xg = grpp.tile([P, 2, cols, 4], BF16, tag="grp", name=name + "g", align_bytes=64)
-            xgw = xg[:].rearrange("p a m e -> p (a m e)").bitcast(F32).rearrange("p (a m u) -> p a m u", a=2, u=2)
-            n = 0
-            for a in range(2):
-                for pr in range(len(tiles) // 2):
-                    bank = ps_t.tile([P, 2, 2, P], F32, tag="tp", name="bank")
-                    for u in range(2):
-                        for i in range(2):
-                            j = 2 * a + u
-                            nc.tensor.transpose(bank[:, u, i, :], tiles[2 * pr + i][:, P * j : P * j + P], ident_f[:])
-                    copy_engines["sv"[n % 2]](
-                        out=xgw[:, a, 256 * pr : 256 * pr + 256, :], in_=bank[:].rearrange("p u i m -> p (i m) u")
-                    )
-                    n += 1
-            xc = const.tile([P, 2, cols], U32, name=name + "c", align_bytes=64)
-            xs = const.tile([P, 2, cols], U8, name=name + "s", align_bytes=64)
+        def word_view(tile_ap):
+            return tile_ap.rearrange("p a m e -> p (a m e)").bitcast(F32).rearrange("p (a m u) -> p a m u", a=2, u=2)
+
+        def transpose_bank(key, srcs, a):
+            bank = ps_t.tile([P, 2, 2, P], F32, tag="tp", name="bank")
+            for u in range(2):
+                for i in range(2):
+                    j = 2 * a + u
+                    nc.tensor.transpose(bank[:, u, i, :], srcs[i][:, P * j : P * j + P], ident_f[:])
+            banks[key] = bank
+
+        def copy_bank(key, dst, who):
+            copy_engines[who](out=dst, in_=banks[key][:].rearrange("p u i m -> p (i m) u"))
+
+        def quantise(name, pool, src, cols, tag):
+            xc = pool.tile([P, 2, cols], U32, name=name + "c", tag=tag + "c", align_bytes=64)
+            xs = pool.tile([P, 2, cols], U8, name=name + "s", tag=tag + "s", align_bytes=64)
             nc.vector.quantize_mx(
                 out=xc[:].rearrange("p a m -> p (a m)").bitcast(FP8X4),
                 scales=xs[:].rearrange("p a m -> p (a m)"),
-                in_=xg[:].rearrange("p a m e -> p (a m e)"),
+                in_=src[:].rearrange("p a m e -> p (a m e)"),
             )
             return xc, xs
 
-        vw = vnat[:].rearrange("p b c -> p (b c)").bitcast(F32)
-        vxc, vxs = prepare_x([vw[:, 512 * i : 512 * i + 512] for i in range(4)], "vx")
-
-        gram = {}
-
-        def pre_norm(w, W, g):
+        def pe_gram(w, g):
             if g == 0:
                 gram[w] = ps_m.tile([P, 512], F32, tag="misc", name="gram")
-            nat = natp.tile([P, 4 * C], BF16, tag="nat", name="nat")
-            nc.sync.dma_start(out=nat[:], in_=W[512 * g : 512 * g + 512, :].rearrange("(p t) c -> p (t c)", t=4))
             for i in range(GRAM_BLOCKS):
-                blk = nat[:, P * i : P * i + P]
+                blk = nat[(w, g)][:, P * i : P * i + P]
                 nc.tensor.matmul(
                     gram[w][:, 0:P],
                     lhsT=blk,
@@ -127,38 +147,50 @@ def tile_bcnet_kernel(tc, v, q, Wv, gv, bv, Wq, gq, bq, h_mat, h_bias, out):
                     start=(g == 0 and i == 0),
                     stop=(g == G - 1 and i == GRAM_BLOCKS - 1),
                 )
+
+        def s_square(w, g):
             nc.scalar.activation(
                 out=junk[:],
-                in_=nat[:, P * GRAM_BLOCKS :],
+                in_=nat[(w, g)][:, P * GRAM_BLOCKS :],
                 func=ACT.Square,
                 accum_out=accs[w][:, P + g : P + g + 1],
             )
-            natw = nat[:].bitcast(F32)
-            grp = grpp.tile([P, 2, 512, 4], BF16, tag="grp", name="grp", align_bytes=64)
-            grpw = grp[:].rearrange("p a m e -> p (a m e)").bitcast(F32).rearrange("p (a m u) -> p a m u", a=2, u=2)
-            n = 0
-            for a in range(2):
-                for hf in range(2):
-                    bank = ps_t.tile([P, 2, 2, P], F32, tag="tp", name="bank")
-                    for u in range(2):
-                        for i in range(2):
-                            t = 2 * hf + i
-                            j = 2 * a + u
-                            nc.tensor.transpose(
-                                bank[:, u, i, :], natw[:, 512 * t + P * j : 512 * t + P * j + P], ident_f[:]
-                            )
-                    copy_engines["s" if n < EVAC_S[w] else "v"](
-                        out=grpw[:, a, 256 * hf : 256 * hf + 256, :], in_=bank[:].rearrange("p u i m -> p (i m) u")
-                    )
-                    n += 1
-            return grp
 
-        def norm_chain(w):
+        def pe_bank(w, g, n):
+            natw = nat[(w, g)][:].bitcast(F32)
+            a, hf = n // 2, n % 2
+            transpose_bank((w, g, n), [natw[:, 512 * (2 * hf + i) : 512 * (2 * hf + i) + 512] for i in range(2)], a)
+
+        def out_bank(w, g, n):
+            if n == 0:
+                grp[(w, g)] = grpp.tile([P, 2, 512, 4], BF16, tag="grp", name="grp", align_bytes=64)
+            a, hf = n // 2, n % 2
+            copy_bank((w, g, n), word_view(grp[(w, g)][:])[:, a, 256 * hf : 256 * hf + 256, :], EVAC[w][n])
+
+        def chunk_pre(w, g):
+            pe_gram(w, g)
+            s_square(w, g)
+            if g == G - 1:
+                chain_mask(w)
+            for n in range(4):
+                pe_bank(w, g, n)
+                out_bank(w, g, n)
+                if g == G - 1 and n == 1:
+                    chain_sum(w)
+            next_load()
+
+        small = {}
+
+        def chain_mask(w):
             nc.vector.tensor_tensor(out=accs[w][:, 0:P], in0=gram[w][:, 0:P], in1=ident_f[:], op=ALU.mult)
-            tot_ps = ps_m.tile([P, 512], F32, tag="misc", name="tot_ps")
-            nc.tensor.matmul(tot_ps[:, 0 : P + 8], lhsT=ones_f[:], rhs=accs[w][:], start=True, stop=True)
+
+        def chain_sum(w):
+            small[w] = ps_m.tile([P, 512], F32, tag="misc", name="tot_ps")
+            nc.tensor.matmul(small[w][:, 0 : P + 8], lhsT=ones_f[:], rhs=accs[w][:], start=True, stop=True)
+
+        def chain_b(w):
             tot = const.tile([P, 1], F32, name="tot_" + w)
-            nc.vector.reduce_sum(out=tot[:], in_=tot_ps[:, 0 : P + 8], axis=AX.X)
+            nc.vector.reduce_sum(out=tot[:], in_=small[w][:, 0 : P + 8], axis=AX.X)
             root = const.tile([P, 1], F32, name="root_" + w)
             nc.scalar.activation(out=root[:], in_=tot[:], func=ACT.Sqrt)
             inv = const.tile([P, 1], F32, name="inv_" + w)
@@ -167,55 +199,36 @@ def tile_bcnet_kernel(tc, v, q, Wv, gv, bv, Wq, gq, bq, h_mat, h_bias, out):
             nc.vector.tensor_tensor(out=s[:], in0=inv[:], in1=g_b[w][:], op=ALU.mult)
             return s
 
-        def scale_chunk(grp, s):
-            flat = grp[:].rearrange("p a m e -> p (a m e)")
+        def scale_chunk(w, g, s):
+            flat = grp[(w, g)][:].rearrange("p a m e -> p (a m e)")
             nc.vector.tensor_scalar(out=flat, in0=flat, scalar1=s[:, 0:1], scalar2=None, op0=ALU.mult)
 
-        def quantise_chunk(grp):
-            wc = codp.tile([P, 2, 512], U32, tag="wc", name="wc", align_bytes=64)
-            ws = codp.tile([P, 2, 512], U8, tag="ws", name="ws", align_bytes=64)
-            nc.vector.quantize_mx(
-                out=wc[:].rearrange("p a m -> p (a m)").bitcast(FP8X4),
-                scales=ws[:].rearrange("p a m -> p (a m)"),
-                in_=grp[:].rearrange("p a m e -> p (a m e)"),
-            )
-            return wc, ws
+        def quantise_chunk(w, g):
+            codes[(w, g)] = quantise("w", codp, grp[(w, g)], 512, "w")
 
-        grps_v = [pre_norm("v", Wv, g) for g in range(G)]
-        s_v = norm_chain("v")
-        qnat = natp.tile([P, B, C], BF16, tag="nat", name="qnat")
-        nc.sync.dma_start(out=qnat[:], in_=q.rearrange("b p c -> p b c"))
+        x_grouped = {}
+        x_codes = {}
 
-        v_sb = const.tile([P, G, 4, B * N], F32, name="v_sb")
+        def x_bank(w, n, who):
+            rows = B * D if w == "q" else B * N
+            if n == 0:
+                x_grouped[w] = grpp.tile([P, 2, rows, 4], BF16, tag="grp", name="xg", align_bytes=64)
+            xw = nat[("x", w)][:].rearrange("p b c -> p (b c)").bitcast(F32)
+            a, b = n // (rows // 256), n % (rows // 256)
+            transpose_bank((w, "x", n), [xw[:, 512 * (2 * b + i) : 512 * (2 * b + i) + 512] for i in range(2)], a)
+            copy_bank((w, "x", n), word_view(x_grouped[w][:])[:, a, 256 * b : 256 * b + 256, :], who)
 
-        def v_project(g):
-            wc, ws = quantise_chunk(grps_v[g])
-            for t in range(4):
-                bank = ps_a.tile([P, B * N], F32, tag="acc", name="vbank")
-                for a in range(2):
-                    nc.tensor.matmul_mx(
-                        out=bank[:],
-                        lhsT=wc[:, a, P * t : P * t + P].bitcast(FP8X4),
-                        lhsT_scale=ws[:, a, P * t : P * t + P],
-                        rhs=vxc[:, a, :].bitcast(FP8X4),
-                        rhs_scale=vxs[:, a, :],
-                        start=(a == 0),
-                        stop=(a == 1),
-                    )
-                nc.scalar.activation(
-                    out=v_sb[:, g, t, :], in_=bank[:], func=ACT.Identity, bias=sm[:, 4 * g + t, 0:1], scale=1.0
-                )
-
-        for i in range(G + 1):
-            if i < G:
-                scale_chunk(grps_v[i], s_v)
-            if i >= 1:
-                v_project(i - 1)
-
-        qw = qnat[:].rearrange("p b c -> p (b c)").bitcast(F32)
-        qxc, qxs = prepare_x([qw[:, 512 * i : 512 * i + 512] for i in range(2)], "qx")
-        grps_q = [pre_norm("q", Wq, g) for g in range(G)]
-        s_q = norm_chain("q")
+        for g in range(G):
+            chunk_pre("q", g)
+            if g == X_AT - 1:
+                x_bank("q", 0, "s")
+                x_bank("q", 1, "v")
+                next_load()
+            if g == X_AT:
+                x_codes["q"] = quantise("qx", const, x_grouped["q"], B * D, "qx")
+            if g == SMALL_AT:
+                bq_f = widen("bq_f", bq_b)
+                hb = widen("hb", hb_b)
 
         qc = const.tile([P, G, B * D], U32, name="qc", align_bytes=64)
         qs = const.tile([P, G, B * D], U8, name="qs", align_bytes=64)
@@ -223,7 +236,7 @@ def tile_bcnet_kernel(tc, v, q, Wv, gv, bv, Wq, gq, bq, h_mat, h_bias, out):
         q_grouped = {}
 
         def q_project(g):
-            wc, ws = quantise_chunk(grps_q[g])
+            wc, ws = codes[("q", g)]
             q_banks[g] = []
             for b in range(B):
                 bank = ps_a.tile([P, 4, D], F32, tag="acc", name="qbank")
@@ -233,8 +246,8 @@ def tile_bcnet_kernel(tc, v, q, Wv, gv, bv, Wq, gq, bq, h_mat, h_bias, out):
                             out=bank[:, t, :],
                             lhsT=wc[:, a, P * t : P * t + P].bitcast(FP8X4),
                             lhsT_scale=ws[:, a, P * t : P * t + P],
-                            rhs=qxc[:, a, D * b : D * b + D].bitcast(FP8X4),
-                            rhs_scale=qxs[:, a, D * b : D * b + D],
+                            rhs=x_codes["q"][0][:, a, D * b : D * b + D].bitcast(FP8X4),
+                            rhs_scale=x_codes["q"][1][:, a, D * b : D * b + D],
                             start=(a == 0),
                             stop=(a == 1),
                         )
@@ -246,7 +259,7 @@ def tile_bcnet_kernel(tc, v, q, Wv, gv, bv, Wq, gq, bq, h_mat, h_bias, out):
                 nc.vector.tensor_tensor(
                     out=qg[:, b, :, :],
                     in0=q_banks[g][b][:].rearrange("p t d -> p d t"),
-                    in1=sm[:, 4 * g : 4 * g + 4, 1].unsqueeze(1).to_broadcast([P, D, 4]),
+                    in1=bq_f[:, 4 * g : 4 * g + 4].unsqueeze(1).to_broadcast([P, D, 4]),
                     op=ALU.add,
                 )
             q_grouped[g] = qg
@@ -258,50 +271,103 @@ def tile_bcnet_kernel(tc, v, q, Wv, gv, bv, Wq, gq, bq, h_mat, h_bias, out):
                 in_=q_grouped[g][:].rearrange("p b d t -> p (b d t)"),
             )
 
-        for i in range(G + 3):
+        s_q = chain_b("q")
+        x_bank("v", 0, "s")
+        x_bank("v", 1, "v")
+        x_bank("v", 2, "s")
+        x_bank("v", 3, "v")
+        next_load()
+        pe_gram("v", 0)
+        scale_chunk("q", 0, s_q)
+        x_codes["v"] = quantise("vx", const, x_grouped["v"], B * N, "vx")
+        for i in range(G + 1):
             if i < G:
-                scale_chunk(grps_q[i], s_q)
-            if 0 <= i - 3 < G:
-                q_quantise(i - 3)
-            if 0 <= i - 2 < G:
-                q_bias(i - 2)
-            if 0 <= i - 1 < G:
-                q_project(i - 1)
+                quantise_chunk("q", i)
+                if i > 0:
+                    pe_gram("v", i)
+                s_square("v", i)
+            if i >= 1:
+                q_bias(i - 1)
+            if i + 1 < G:
+                scale_chunk("q", i + 1, s_q)
+            if i >= 1:
+                q_quantise(i - 1)
+            if i < G:
+                for n in range(4):
+                    pe_bank("v", i, n)
+                    out_bank("v", i, n)
+                    if i == G - 1 and n == 0:
+                        chain_mask("v")
+                    if i == G - 1 and n == 1:
+                        chain_sum("v")
+                next_load()
+                q_project(i)
+        bv_f = widen("bv_f", late["bv"])
+        s_v = chain_b("v")
+
+        v_sb = const.tile([P, G, 4, B * N], F32, name="v_sb")
+
+        def v_project(g):
+            wc, ws = codes[("v", g)]
+            for t in range(4):
+                bank = ps_a.tile([P, B * N], F32, tag="acc", name="vbank")
+                for a in range(2):
+                    nc.tensor.matmul_mx(
+                        out=bank[:],
+                        lhsT=wc[:, a, P * t : P * t + P].bitcast(FP8X4),
+                        lhsT_scale=ws[:, a, P * t : P * t + P],
+                        rhs=x_codes["v"][0][:, a, :].bitcast(FP8X4),
+                        rhs_scale=x_codes["v"][1][:, a, :],
+                        start=(a == 0),
+                        stop=(a == 1),
+                    )
+                nc.scalar.activation(
+                    out=v_sb[:, g, t, :], in_=bank[:], func=ACT.Identity, bias=bv_f[:, 4 * g + t : 4 * g + t + 1], scale=1.0
+                )
 
         head_codes = {}
         pair_tiles = {}
+        planar = {}
+        lg_tiles = {}
 
-        def hv_unit(h, gp, j):
-            g = 2 * gp + j
+        def s_mult(h, g):
+            if g in VPATH[h]:
+                return
+            hp = hpp.tile([P, 4, B * N], BF16, tag="hp", name="hp")
+            for t in range(4):
+                nc.scalar.activation(
+                    out=hp[:, t, :], in_=v_sb[:, g, t, :], func=ACT.Copy, scale=hm_f[:, 4 * (G * h + g) + t : 4 * (G * h + g) + t + 1]
+                )
+            planar[(h, g)] = hp
+
+        def v_group(h, g):
+            gp, j = g // 2, g % 2
+            if g == 0:
+                hc_t = hcp.tile([P, G, B * N], U32, tag="hc", name="hc_t", align_bytes=64)
+                hs_t = hcp.tile([P, G, B * N], U8, tag="hs", name="hs_t", align_bytes=64)
+                head_codes[h] = (hc_t, hs_t)
+            if j == 0:
+                pair_tiles[(h, gp)] = grpp.tile([P, 2, B * N, 4], BF16, tag="grp", name="hg_t", align_bytes=64)
             hg = pair_tiles[(h, gp)]
             if g in VPATH[h]:
                 nc.vector.tensor_tensor(
                     out=hg[:, j, :, :],
                     in0=v_sb[:, g, :, :].rearrange("p t n -> p n t"),
-                    in1=sm[:, 4 * g : 4 * g + 4, 2 + h].unsqueeze(1).to_broadcast([P, B * N, 4]),
+                    in1=hm_f[:, 4 * (G * h + g) : 4 * (G * h + g) + 4].unsqueeze(1).to_broadcast([P, B * N, 4]),
                     op=ALU.mult,
                 )
             else:
-                hp = hpp.tile([P, 4, B * N], BF16, tag="hp", name="hp")
-                for t in range(4):
-                    nc.scalar.activation(
-                        out=hp[:, t, :],
-                        in_=v_sb[:, g, t, :],
-                        func=ACT.Copy,
-                        scale=sm[:, 4 * g + t, 2 + h : 3 + h],
-                    )
                 nc.vector.tensor_copy(
                     out=hg[:, j, :, :].rearrange("p (c i) t -> p c t i", i=4),
-                    in_=hp[:].rearrange("p t (c i) -> p c t i", i=4),
+                    in_=planar[(h, g)][:].rearrange("p t (c i) -> p c t i", i=4),
                 )
 
         def hv_quantise(h, gp):
             hc, hs = head_codes[h]
-            hg = pair_tiles[(h, gp)]
             nc.vector.quantize_mx(
                 out=hc[:, 2 * gp : 2 * gp + 2, :].rearrange("p g n -> p (g n)").bitcast(FP8X4),
                 scales=hs[:, 2 * gp : 2 * gp + 2, :].rearrange("p g n -> p (g n)"),
-                in_=hg[:].rearrange("p j n t -> p (j n t)"),
+                in_=pair_tiles[(h, gp)][:].rearrange("p j n t -> p (j n t)"),
             )
 
         def logits(h):
@@ -319,27 +385,35 @@ def tile_bcnet_kernel(tc, v, q, Wv, gv, bv, Wq, gq, bq, h_mat, h_bias, out):
                         start=(g == 0),
                         stop=(g == G - 1),
                     )
+            lg_tiles[h] = lg
+
+        def store(h):
             o_sb = outp.tile([P, 4, D], F32, tag="o", name="o_sb")
-            nc.scalar.activation(out=o_sb[:], in_=lg[:], func=ACT.Identity, bias=hb[:, h : h + 1], scale=1.0)
+            nc.scalar.activation(out=o_sb[:], in_=lg_tiles[h][:], func=ACT.Identity, bias=hb[:, h : h + 1], scale=1.0)
             nc.sync.dma_start(
                 out=out[:, h].rearrange("b (m r) d -> m b (r d)", r=2),
                 in_=o_sb[:].rearrange("p (b r) d -> p b (r d)", b=2),
             )
 
-        pairs = [(h, gp) for h in range(H) for gp in range(G // 2)]
-        for i in range(len(pairs) + 1):
-            if i < len(pairs):
-                h, gp = pairs[i]
-                if gp == 0:
-                    hc_t = hcp.tile([P, G, B * N], U32, tag="hc", name="hc_t", align_bytes=64)
-                    hs_t = hcp.tile([P, G, B * N], U8, tag="hs", name="hs_t", align_bytes=64)
-                    head_codes[h] = (hc_t, hs_t)
-                hg_t = grpp.tile([P, 2, B * N, 4], BF16, tag="grp", name="hg_t", align_bytes=64)
-                pair_tiles[(h, gp)] = hg_t
-                hv_unit(h, gp, 0)
-            if i >= 1:
-                hv_quantise(pairs[i - 1][0], pairs[i - 1][1])
-                if pairs[i - 1][1] == G // 2 - 1:
-                    logits(pairs[i - 1][0])
-            if i < len(pairs):
-                hv_unit(pairs[i][0], pairs[i][1], 1)
+        units = [(h, g) for h in range(H) for g in range(G)]
+        U = len(units)
+        scale_chunk("v", 0, s_v)
+        hm_f = widen("hm_f", late["hm"])
+        for i in range(U + S_AHEAD + 1):
+            if i + 1 < G:
+                scale_chunk("v", i + 1, s_v)
+            if i < G:
+                quantise_chunk("v", i)
+                v_project(i)
+            if i < U:
+                s_mult(units[i][0], units[i][1])
+                if units[i][1] == EVAC_LAG and units[i][0] >= 1:
+                    store(units[i][0] - 1)
+            k = i - S_AHEAD
+            if 0 <= k < U:
+                v_group(units[k][0], units[k][1])
+            if 0 <= k - 1 < U and units[k - 1][1] % 2 == 1:
+                hv_quantise(units[k - 1][0], units[k - 1][1] // 2)
+                if units[k - 1][1] == G - 1:
+                    logits(units[k - 1][0])
+        store(H - 1)

@@ -22,7 +22,7 @@ NAT_BUFS = 4
 X_AT = 3
 SMALL_AT = 4
 EVAC = {"q": "vvvv", "v": "sssv"}
-VPATH = ((2, 5), (0,), (0,), (0,), (0,), (0,), (0,), (0,))
+VPATH = ((2, 5), (0, 3), (0, 3), (0, 3), (0, 3), (0, 3), (0, 3), (0,))
 S_AHEAD = 2
 EVAC_LAG = 4
 

@@ -17,12 +17,12 @@ B, N, D, C, K, H = 2, 256, 128, 1024, 3072, 8
 G = K // 512
 FLOPS = 2 * (B * N * K * C + B * D * K * C + B * H * N * D * K)
 
-GRAM_BLOCKS = 15
+GRAM_BLOCKS = {"q": (15, 16, 16, 16, 16, 16), "v": (15, 15, 16, 16, 16, 16)}
 NAT_BUFS = 4
 X_AT = 3
 SMALL_AT = 4
-EVAC = {"q": "vvvv", "v": "sssv"}
-VPATH = ((2, 5), (0, 3), (0, 3), (0, 3), (0, 3), (0, 3), (0, 3), (0,))
+EVAC = {"q": ("vvvv",) * 6, "v": ("sssv",) * 6}
+VPATH = ((2, 5), (0,), (0,), (0,), (0,), (0,), (0,), (0,))
 S_AHEAD = 2
 EVAC_LAG = 4
 
@@ -107,7 +107,7 @@ def tile_bcnet_kernel(tc, v, q, Wv, gv, bv, Wq, gq, bq, h_mat, h_bias, out):
         for w in ("q", "v"):
             accs[w] = const.tile([P, P + 8], F32, name="accs_" + w)
             nc.vector.memset(accs[w][:], 0.0)
-        junk = const.tile([P, 4096 - P * GRAM_BLOCKS], BF16, name="junk")
+        junk = const.tile([P, 4096 - P * 15], BF16, name="junk")
 
         copy_engines = {"s": nc.scalar.copy, "v": nc.vector.tensor_copy}
 
@@ -138,20 +138,21 @@ def tile_bcnet_kernel(tc, v, q, Wv, gv, bv, Wq, gq, bq, h_mat, h_bias, out):
         def pe_gram(w, g):
             if g == 0:
                 gram[w] = ps_m.tile([P, 512], F32, tag="misc", name="gram")
-            for i in range(GRAM_BLOCKS):
+            for i in range(GRAM_BLOCKS[w][g]):
                 blk = nat[(w, g)][:, P * i : P * i + P]
                 nc.tensor.matmul(
                     gram[w][:, 0:P],
                     lhsT=blk,
                     rhs=blk,
                     start=(g == 0 and i == 0),
-                    stop=(g == G - 1 and i == GRAM_BLOCKS - 1),
+                    stop=(g == G - 1 and i == GRAM_BLOCKS[w][g] - 1),
                 )
 
         def s_square(w, g):
+            first = P * GRAM_BLOCKS[w][g]
             nc.scalar.activation(
-                out=junk[:],
-                in_=nat[(w, g)][:, P * GRAM_BLOCKS :],
+                out=junk[:, 0 : 4096 - first],
+                in_=nat[(w, g)][:, first:],
                 func=ACT.Square,
                 accum_out=accs[w][:, P + g : P + g + 1],
             )
@@ -165,7 +166,7 @@ def tile_bcnet_kernel(tc, v, q, Wv, gv, bv, Wq, gq, bq, h_mat, h_bias, out):
             if n == 0:
                 grp[(w, g)] = grpp.tile([P, 2, 512, 4], BF16, tag="grp", name="grp", align_bytes=64)
             a, hf = n // 2, n % 2
-            copy_bank((w, g, n), word_view(grp[(w, g)][:])[:, a, 256 * hf : 256 * hf + 256, :], EVAC[w][n])
+            copy_bank((w, g, n), word_view(grp[(w, g)][:])[:, a, 256 * hf : 256 * hf + 256, :], EVAC[w][g][n])
 
         def chunk_pre(w, g):
             pe_gram(w, g)
@@ -286,6 +287,8 @@ def tile_bcnet_kernel(tc, v, q, Wv, gv, bv, Wq, gq, bq, h_mat, h_bias, out):
                 if i > 0:
                     pe_gram("v", i)
                 s_square("v", i)
+                if i == G - 1:
+                    chain_mask("v")
             if i >= 1:
                 q_bias(i - 1)
             if i + 1 < G:
@@ -296,21 +299,24 @@ def tile_bcnet_kernel(tc, v, q, Wv, gv, bv, Wq, gq, bq, h_mat, h_bias, out):
                 for n in range(4):
                     pe_bank("v", i, n)
                     out_bank("v", i, n)
-                    if i == G - 1 and n == 0:
-                        chain_mask("v")
                     if i == G - 1 and n == 1:
                         chain_sum("v")
                 next_load()
+                if i == G - 1:
+                    s_v = chain_b("v")
+                    scale_chunk("v", 0, s_v)
+                    bv_f = widen("bv_f", late["bv"])
+                    hm_f = widen("hm_f", late["hm"])
+                    quantise_chunk("v", 0)
+                    scale_chunk("v", 1, s_v)
                 q_project(i)
-        bv_f = widen("bv_f", late["bv"])
-        s_v = chain_b("v")
 
         v_sb = const.tile([P, G, 4, B * N], F32, name="v_sb")
 
         def v_project(g):
             wc, ws = codes[("v", g)]
             for t in range(4):
-                bank = ps_a.tile([P, B * N], F32, tag="acc", name="vbank")
+                bank = ps_t.tile([P, B * N], F32, tag="tp", name="vbank")
                 for a in range(2):
                     nc.tensor.matmul_mx(
                         out=bank[:],
@@ -387,6 +393,44 @@ def tile_bcnet_kernel(tc, v, q, Wv, gv, bv, Wq, gq, bq, h_mat, h_bias, out):
                     )
             lg_tiles[h] = lg
 
+        last_banks = []
+
+        def last_logits(gp):
+            hc, hs = head_codes[H - 1]
+            if gp == 0:
+                for br in range(4):
+                    pool, tag = (ps_t, "tp") if br < 3 else (ps_a, "acc")
+                    last_banks.append(pool.tile([P, D], F32, tag=tag, name="lg_last"))
+            for br in range(4):
+                b = br // 2
+                for g in (2 * gp, 2 * gp + 1):
+                    nc.tensor.matmul_mx(
+                        out=last_banks[br][:],
+                        lhsT=hc[:, g, P * br : P * br + P].bitcast(FP8X4),
+                        lhsT_scale=hs[:, g, P * br : P * br + P],
+                        rhs=qc[:, g, D * b : D * b + D].bitcast(FP8X4),
+                        rhs_scale=qs[:, g, D * b : D * b + D],
+                        start=(g == 0),
+                        stop=(g == G - 1),
+                    )
+
+        def last_store():
+            h = H - 1
+            for b in range(B):
+                o_sb = outp.tile([P, 2, D], F32, tag="o", name="o_last")
+                for r in range(2):
+                    if b == 0:
+                        nc.scalar.activation(
+                            out=o_sb[:, r, :], in_=last_banks[r][:], func=ACT.Identity, bias=hb[:, h : h + 1], scale=1.0
+                        )
+                    else:
+                        nc.vector.tensor_scalar(
+                            out=o_sb[:, r, :], in0=last_banks[2 + r][:], scalar1=hb[:, h : h + 1], scalar2=None, op0=ALU.add
+                        )
+                nc.sync.dma_start(
+                    out=out[b, h].rearrange("(m r) d -> m (r d)", r=2), in_=o_sb[:].rearrange("p r d -> p (r d)")
+                )
+
         def store(h):
             o_sb = outp.tile([P, 4, D], F32, tag="o", name="o_sb")
             nc.scalar.activation(out=o_sb[:], in_=lg_tiles[h][:], func=ACT.Identity, bias=hb[:, h : h + 1], scale=1.0)
@@ -397,13 +441,12 @@ def tile_bcnet_kernel(tc, v, q, Wv, gv, bv, Wq, gq, bq, h_mat, h_bias, out):
 
         units = [(h, g) for h in range(H) for g in range(G)]
         U = len(units)
-        scale_chunk("v", 0, s_v)
-        hm_f = widen("hm_f", late["hm"])
         for i in range(U + S_AHEAD + 1):
-            if i + 1 < G:
+            if 1 <= i and i + 1 < G:
                 scale_chunk("v", i + 1, s_v)
             if i < G:
-                quantise_chunk("v", i)
+                if i >= 1:
+                    quantise_chunk("v", i)
                 v_project(i)
             if i < U:
                 s_mult(units[i][0], units[i][1])
@@ -414,6 +457,8 @@ def tile_bcnet_kernel(tc, v, q, Wv, gv, bv, Wq, gq, bq, h_mat, h_bias, out):
                 v_group(units[k][0], units[k][1])
             if 0 <= k - 1 < U and units[k - 1][1] % 2 == 1:
                 hv_quantise(units[k - 1][0], units[k - 1][1] // 2)
-                if units[k - 1][1] == G - 1:
+                if units[k - 1][0] == H - 1:
+                    last_logits(units[k - 1][1] // 2)
+                elif units[k - 1][1] == G - 1:
                     logits(units[k - 1][0])
-        store(H - 1)
+        last_store()

@@ -23,6 +23,7 @@ X_AT = 3
 SMALL_AT = 4
 EVAC = {"q": ("vvvv",) * 6, "v": ("sssv",) * 6}
 VPATH = ((2, 5), (0,), (0,), (0,), (0,), (0,), (0,), (0,))
+SCALE_ON_S = ()
 S_AHEAD = 2
 EVAC_LAG = 4
 
@@ -202,7 +203,10 @@ def tile_bcnet_kernel(tc, v, q, Wv, gv, bv, Wq, gq, bq, h_mat, h_bias, out):
 
         def scale_chunk(w, g, s):
             flat = grp[(w, g)][:].rearrange("p a m e -> p (a m e)")
-            nc.vector.tensor_scalar(out=flat, in0=flat, scalar1=s[:, 0:1], scalar2=None, op0=ALU.mult)
+            if (w, g) in SCALE_ON_S:
+                nc.scalar.activation(out=flat, in_=flat, func=ACT.Copy, scale=s[:, 0:1])
+            else:
+                nc.vector.tensor_scalar(out=flat, in0=flat, scalar1=s[:, 0:1], scalar2=None, op0=ALU.mult)
 
         def quantise_chunk(w, g):
             codes[(w, g)] = quantise("w", codp, grp[(w, g)], 512, "w")
@@ -258,9 +262,9 @@ def tile_bcnet_kernel(tc, v, q, Wv, gv, bv, Wq, gq, bq, h_mat, h_bias, out):
             qg = codp.tile([P, B, D, 4], BF16, tag="qg", name="qg", align_bytes=64, bufs=2)
             for b in range(B):
                 nc.vector.tensor_tensor(
-                    out=qg[:, b, :, :],
-                    in0=q_banks[g][b][:].rearrange("p t d -> p d t"),
-                    in1=bq_f[:, 4 * g : 4 * g + 4].unsqueeze(1).to_broadcast([P, D, 4]),
+                    out=qg[:, b, :, :].rearrange("p (c i) t -> p c t i", i=4),
+                    in0=q_banks[g][b][:].rearrange("p t (c i) -> p c t i", i=4),
+                    in1=bq_f[:, 4 * g : 4 * g + 4].unsqueeze(1).unsqueeze(3).to_broadcast([P, D // 4, 4, 4]),
                     op=ALU.add,
                 )
             q_grouped[g] = qg
@@ -357,9 +361,12 @@ def tile_bcnet_kernel(tc, v, q, Wv, gv, bv, Wq, gq, bq, h_mat, h_bias, out):
             hg = pair_tiles[(h, gp)]
             if g in VPATH[h]:
                 nc.vector.tensor_tensor(
-                    out=hg[:, j, :, :],
-                    in0=v_sb[:, g, :, :].rearrange("p t n -> p n t"),
-                    in1=hm_f[:, 4 * (G * h + g) : 4 * (G * h + g) + 4].unsqueeze(1).to_broadcast([P, B * N, 4]),
+                    out=hg[:, j, :, :].rearrange("p (c i) t -> p c t i", i=4),
+                    in0=v_sb[:, g, :, :].rearrange("p t (c i) -> p c t i", i=4),
+                    in1=hm_f[:, 4 * (G * h + g) : 4 * (G * h + g) + 4]
+                    .unsqueeze(1)
+                    .unsqueeze(3)
+                    .to_broadcast([P, B * N // 4, 4, 4]),
                     op=ALU.mult,
                 )
             else:

@@ -19,11 +19,12 @@ FLOPS = 2 * (B * N * K * C + B * D * K * C + B * H * N * D * K)
 
 GRAM_BLOCKS = {"q": (15, 16, 16, 16, 16, 16), "v": (15, 15, 16, 16, 16, 16)}
 NAT_BUFS = 4
+GRP_BUFS = 8
 X_AT = 3
 SMALL_AT = 4
 EVAC = {"q": ("vvvv",) * 6, "v": ("sssv",) * 6}
 VPATH = ((2, 5), (0,), (0,), (0,), (0,), (0,), (0,), (0,))
-SCALE_ON_S = ()
+X_EVAC = "ssss"
 S_AHEAD = 2
 EVAC_LAG = 4
 
@@ -33,9 +34,8 @@ def tile_bcnet_kernel(tc, v, q, Wv, gv, bv, Wq, gq, bq, h_mat, h_bias, out):
     with ExitStack() as ctx:
         const = ctx.enter_context(tc.tile_pool(name="const", bufs=1))
         natp = ctx.enter_context(tc.tile_pool(name="natp", bufs=NAT_BUFS))
-        hpp = ctx.enter_context(tc.tile_pool(name="hpp", bufs=S_AHEAD + 1))
-        grpp = ctx.enter_context(tc.tile_pool(name="grpp", bufs=8))
-        codp = ctx.enter_context(tc.tile_pool(name="codp", bufs=3))
+        grpp = ctx.enter_context(tc.tile_pool(name="grpp", bufs=GRP_BUFS))
+        codp = ctx.enter_context(tc.tile_pool(name="codp", bufs=2))
         hcp = ctx.enter_context(tc.tile_pool(name="hcp", bufs=2))
         outp = ctx.enter_context(tc.tile_pool(name="outp", bufs=2))
         ps_t = ctx.enter_context(tc.psum_pool(name="ps_t", bufs=3))
@@ -202,11 +202,15 @@ def tile_bcnet_kernel(tc, v, q, Wv, gv, bv, Wq, gq, bq, h_mat, h_bias, out):
             return s
 
         def scale_chunk(w, g, s):
-            flat = grp[(w, g)][:].rearrange("p a m e -> p (a m e)")
-            if (w, g) in SCALE_ON_S:
-                nc.scalar.activation(out=flat, in_=flat, func=ACT.Copy, scale=s[:, 0:1])
-            else:
-                nc.vector.tensor_scalar(out=flat, in0=flat, scalar1=s[:, 0:1], scalar2=None, op0=ALU.mult)
+            raw = grp[(w, g)]
+            grp[(w, g)] = grpp.tile([P, 2, 512, 4], BF16, tag="scl", name="scaled", align_bytes=64, bufs=2)
+            nc.vector.tensor_scalar(
+                out=grp[(w, g)][:].rearrange("p a m e -> p (a m e)"),
+                in0=raw[:].rearrange("p a m e -> p (a m e)"),
+                scalar1=s[:, 0:1],
+                scalar2=None,
+                op0=ALU.mult,
+            )
 
         def quantise_chunk(w, g):
             codes[(w, g)] = quantise("w", codp, grp[(w, g)], 512, "w")
@@ -277,10 +281,8 @@ def tile_bcnet_kernel(tc, v, q, Wv, gv, bv, Wq, gq, bq, h_mat, h_bias, out):
             )
 
         s_q = chain_b("q")
-        x_bank("v", 0, "s")
-        x_bank("v", 1, "v")
-        x_bank("v", 2, "s")
-        x_bank("v", 3, "v")
+        for n in range(4):
+            x_bank("v", n, X_EVAC[n])
         next_load()
         pe_gram("v", 0)
         scale_chunk("q", 0, s_q)
@@ -343,7 +345,7 @@ def tile_bcnet_kernel(tc, v, q, Wv, gv, bv, Wq, gq, bq, h_mat, h_bias, out):
         def s_mult(h, g):
             if g in VPATH[h]:
                 return
-            hp = hpp.tile([P, 4, B * N], BF16, tag="hp", name="hp")
+            hp = natp.tile([P, 4, B * N], BF16, tag="nat", name="hp")
             for t in range(4):
                 nc.scalar.activation(
                     out=hp[:, t, :], in_=v_sb[:, g, t, :], func=ACT.Copy, scale=hm_f[:, 4 * (G * h + g) + t : 4 * (G * h + g) + t + 1]

@@ -17,7 +17,7 @@ B, N, D, C, K, H = 2, 256, 128, 1024, 3072, 8
 G = K // 512
 FLOPS = 2 * (B * N * K * C + B * D * K * C + B * H * N * D * K)
 
-GRAM_BLOCKS = {"q": (15, 16, 16, 16, 16, 16), "v": (15, 15, 16, 16, 16, 16)}
+GRAM_BLOCKS = {"q": (10,) * 6, "v": (12,) * 6}
 NAT_BUFS = 4
 GRP_BUFS = 8
 X_AT = 3
@@ -108,7 +108,7 @@ def tile_bcnet_kernel(tc, v, q, Wv, gv, bv, Wq, gq, bq, h_mat, h_bias, out):
         for w in ("q", "v"):
             accs[w] = const.tile([P, P + 8], F32, name="accs_" + w)
             nc.vector.memset(accs[w][:], 0.0)
-        junk = const.tile([P, 4096 - P * 15], BF16, name="junk")
+        junk = const.tile([P, 4096 - P * 10], BF16, name="junk")
 
         copy_engines = {"s": nc.scalar.copy, "v": nc.vector.tensor_copy}
 

from contextlib import ExitStack

import concourse.mybir as mybir
from concourse.masks import make_identity

F32 = mybir.dt.float32
BF16 = mybir.dt.bfloat16
U32 = mybir.dt.uint32
U8 = mybir.dt.uint8
FP8X4 = mybir.dt.float8_e4m3fn_x4
ACT = mybir.ActivationFunctionType
ALU = mybir.AluOpType
AX = mybir.AxisListType

P = 128
B, N, D, C, K, H = 2, 256, 128, 1024, 3072, 8
G = K // 512
FLOPS = 2 * (B * N * K * C + B * D * K * C + B * H * N * D * K)

GRAM_BLOCKS = {"q": (10,) * 6, "v": (12,) * 6}
NAT_BUFS = 4
GRP_BUFS = 8
X_AT = 3
SMALL_AT = 4
EVAC = {"q": ("vvvv",) * 6, "v": ("sssv",) * 6}
VPATH = ((2, 5), (0,), (0,), (0,), (0,), (0,), (0,), (0,))
X_EVAC = "ssss"
S_AHEAD = 2
EVAC_LAG = 4


def tile_bcnet_kernel(tc, v, q, Wv, gv, bv, Wq, gq, bq, h_mat, h_bias, out):
    nc = tc.nc
    with ExitStack() as ctx:
        const = ctx.enter_context(tc.tile_pool(name="const", bufs=1))
        natp = ctx.enter_context(tc.tile_pool(name="natp", bufs=NAT_BUFS))
        grpp = ctx.enter_context(tc.tile_pool(name="grpp", bufs=GRP_BUFS))
        codp = ctx.enter_context(tc.tile_pool(name="codp", bufs=2))
        hcp = ctx.enter_context(tc.tile_pool(name="hcp", bufs=2))
        outp = ctx.enter_context(tc.tile_pool(name="outp", bufs=2))
        ps_t = ctx.enter_context(tc.psum_pool(name="ps_t", bufs=3))
        ps_m = ctx.enter_context(tc.psum_pool(name="ps_m", bufs=3))
        ps_a = ctx.enter_context(tc.psum_pool(name="ps_a", bufs=2))
        ctx.enter_context(tc.manual_schedule())

        W_in = {"q": Wq, "v": Wv}
        nat = {}
        grp = {}
        banks = {}
        gram = {}
        codes = {}

        loads = [("q", g) for g in range(G)] + [("x", "v")] + [("v", g) for g in range(G)]
        loads = loads[:X_AT] + [("x", "q")] + loads[X_AT:]
        issued = [0]

        late = {}

        def next_load():
            if issued[0] == len(loads):
                if not late:
                    late["bv"] = spread("bv", bv.rearrange("(g p t) -> p g t", p=P, t=4), 1, nc.sync)
                    late["hm"] = spread("hm", h_mat.rearrange("a h b (g p t) -> p (a h b g) t", p=P, t=4), H, nc.sync)
                return
            w, g = loads[issued[0]]
            issued[0] += 1
            if w == "x":
                src = q.rearrange("b p c -> p b c") if g == "q" else v.rearrange("b (p r) c -> p b (r c)", r=2)
                nat[(w, g)] = natp.tile([P, B, src.shape[2]], BF16, tag="nat", name="xnat")
                nc.sync.dma_start(out=nat[(w, g)][:], in_=src)
            else:
                nat[(w, g)] = natp.tile([P, 4 * C], BF16, tag="nat", name="nat")
                nc.sync.dma_start(
                    out=nat[(w, g)][:], in_=W_in[w][512 * g : 512 * g + 512, :].rearrange("(p t) c -> p (t c)", t=4)
                )

        for g in range(NAT_BUFS):
            next_load()

        warm = const.tile([P, 1], F32, name="warm")
        nc.vector.memset(warm[:], 1.0)
        warm2 = const.tile([P, 1], F32, name="warm2")
        nc.scalar.activation(out=warm2[:], in_=warm[:], func=ACT.Sqrt)

        def spread(name, src, rows, queue):
            raw = const.tile([P, rows * 4 * G], BF16, name=name + "_b")
            queue.dma_start(out=raw[:].rearrange("p (r t) -> p r t", t=4), in_=src)
            return raw

        def widen(name, raw):
            wide = const.tile([P, raw.shape[1]], F32, name=name)
            nc.vector.tensor_copy(out=wide[:], in_=raw[:])
            return wide

        bq_b = spread("bq", bq.rearrange("(g p t) -> p g t", p=P, t=4), 1, nc.scalar)
        g_b = {}
        for w, g_in in (("q", gq), ("v", gv)):
            g_b[w] = const.tile([P, 1], BF16, name="g_b_" + w)
            nc.scalar.dma_start(out=g_b[w][:], in_=g_in.partition_broadcast(P))
        hb_b = const.tile([P, H], BF16, name="hb_b")
        nc.scalar.dma_start(out=hb_b[:], in_=h_bias.rearrange("a h b c -> (a h b c)").partition_broadcast(P))

        ident_f = const.tile([P, P], F32, name="ident_f")
        make_identity(nc, ident_f[:])
        ones_f = const.tile([P, P], F32, name="ones_f")
        nc.vector.memset(ones_f[:], 1.0)
        accs = {}
        for w in ("q", "v"):
            accs[w] = const.tile([P, P + 8], F32, name="accs_" + w)
            nc.vector.memset(accs[w][:], 0.0)
        junk = const.tile([P, 4096 - P * 10], BF16, name="junk")

        copy_engines = {"s": nc.scalar.copy, "v": nc.vector.tensor_copy}

        def word_view(tile_ap):
            return tile_ap.rearrange("p a m e -> p (a m e)").bitcast(F32).rearrange("p (a m u) -> p a m u", a=2, u=2)

        def transpose_bank(key, srcs, a):
            bank = ps_t.tile([P, 2, 2, P], F32, tag="tp", name="bank")
            for u in range(2):
                for i in range(2):
                    j = 2 * a + u
                    nc.tensor.transpose(bank[:, u, i, :], srcs[i][:, P * j : P * j + P], ident_f[:])
            banks[key] = bank

        def copy_bank(key, dst, who):
            copy_engines[who](out=dst, in_=banks[key][:].rearrange("p u i m -> p (i m) u"))

        def quantise(name, pool, src, cols, tag):
            xc = pool.tile([P, 2, cols], U32, name=name + "c", tag=tag + "c", align_bytes=64)
            xs = pool.tile([P, 2, cols], U8, name=name + "s", tag=tag + "s", align_bytes=64)
            nc.vector.quantize_mx(
                out=xc[:].rearrange("p a m -> p (a m)").bitcast(FP8X4),
                scales=xs[:].rearrange("p a m -> p (a m)"),
                in_=src[:].rearrange("p a m e -> p (a m e)"),
            )
            return xc, xs

        def pe_gram(w, g):
            if g == 0:
                gram[w] = ps_m.tile([P, 512], F32, tag="misc", name="gram")
            for i in range(GRAM_BLOCKS[w][g]):
                blk = nat[(w, g)][:, P * i : P * i + P]
                nc.tensor.matmul(
                    gram[w][:, 0:P],
                    lhsT=blk,
                    rhs=blk,
                    start=(g == 0 and i == 0),
                    stop=(g == G - 1 and i == GRAM_BLOCKS[w][g] - 1),
                )

        def s_square(w, g):
            first = P * GRAM_BLOCKS[w][g]
            nc.scalar.activation(
                out=junk[:, 0 : 4096 - first],
                in_=nat[(w, g)][:, first:],
                func=ACT.Square,
                accum_out=accs[w][:, P + g : P + g + 1],
            )

        def pe_bank(w, g, n):
            natw = nat[(w, g)][:].bitcast(F32)
            a, hf = n // 2, n % 2
            transpose_bank((w, g, n), [natw[:, 512 * (2 * hf + i) : 512 * (2 * hf + i) + 512] for i in range(2)], a)

        def out_bank(w, g, n):
            if n == 0:
                grp[(w, g)] = grpp.tile([P, 2, 512, 4], BF16, tag="grp", name="grp", align_bytes=64)
            a, hf = n // 2, n % 2
            copy_bank((w, g, n), word_view(grp[(w, g)][:])[:, a, 256 * hf : 256 * hf + 256, :], EVAC[w][g][n])

        def chunk_pre(w, g):
            pe_gram(w, g)
            s_square(w, g)
            if g == G - 1:
                chain_mask(w)
            for n in range(4):
                pe_bank(w, g, n)
                out_bank(w, g, n)
                if g == G - 1 and n == 1:
                    chain_sum(w)
            next_load()

        small = {}

        def chain_mask(w):
            nc.vector.tensor_tensor(out=accs[w][:, 0:P], in0=gram[w][:, 0:P], in1=ident_f[:], op=ALU.mult)

        def chain_sum(w):
            small[w] = ps_m.tile([P, 512], F32, tag="misc", name="tot_ps")
            nc.tensor.matmul(small[w][:, 0 : P + 8], lhsT=ones_f[:], rhs=accs[w][:], start=True, stop=True)

        def chain_b(w):
            tot = const.tile([P, 1], F32, name="tot_" + w)
            nc.vector.reduce_sum(out=tot[:], in_=small[w][:, 0 : P + 8], axis=AX.X)
            root = const.tile([P, 1], F32, name="root_" + w)
            nc.scalar.activation(out=root[:], in_=tot[:], func=ACT.Sqrt)
            inv = const.tile([P, 1], F32, name="inv_" + w)
            nc.vector.reciprocal(out=inv[:], in_=root[:])
            s = const.tile([P, 1], F32, name="s_" + w)
            nc.vector.tensor_tensor(out=s[:], in0=inv[:], in1=g_b[w][:], op=ALU.mult)
            return s

        def scale_chunk(w, g, s):
            raw = grp[(w, g)]
            grp[(w, g)] = grpp.tile([P, 2, 512, 4], BF16, tag="scl", name="scaled", align_bytes=64, bufs=2)
            nc.vector.tensor_scalar(
                out=grp[(w, g)][:].rearrange("p a m e -> p (a m e)"),
                in0=raw[:].rearrange("p a m e -> p (a m e)"),
                scalar1=s[:, 0:1],
                scalar2=None,
                op0=ALU.mult,
            )

        def quantise_chunk(w, g):
            codes[(w, g)] = quantise("w", codp, grp[(w, g)], 512, "w")

        x_grouped = {}
        x_codes = {}

        def x_bank(w, n, who):
            rows = B * D if w == "q" else B * N
            if n == 0:
                x_grouped[w] = grpp.tile([P, 2, rows, 4], BF16, tag="grp", name="xg", align_bytes=64)
            xw = nat[("x", w)][:].rearrange("p b c -> p (b c)").bitcast(F32)
            a, b = n // (rows // 256), n % (rows // 256)
            transpose_bank((w, "x", n), [xw[:, 512 * (2 * b + i) : 512 * (2 * b + i) + 512] for i in range(2)], a)
            copy_bank((w, "x", n), word_view(x_grouped[w][:])[:, a, 256 * b : 256 * b + 256, :], who)

        for g in range(G):
            chunk_pre("q", g)
            if g == X_AT - 1:
                x_bank("q", 0, "s")
                x_bank("q", 1, "v")
                next_load()
            if g == X_AT:
                x_codes["q"] = quantise("qx", const, x_grouped["q"], B * D, "qx")
            if g == SMALL_AT:
                bq_f = widen("bq_f", bq_b)
                hb = widen("hb", hb_b)

        qc = const.tile([P, G, B * D], U32, name="qc", align_bytes=64)
        qs = const.tile([P, G, B * D], U8, name="qs", align_bytes=64)
        q_banks = {}
        q_grouped = {}

        def q_project(g):
            wc, ws = codes[("q", g)]
            q_banks[g] = []
            for b in range(B):
                bank = ps_a.tile([P, 4, D], F32, tag="acc", name="qbank")
                for t in range(4):
                    for a in range(2):
                        nc.tensor.matmul_mx(
                            out=bank[:, t, :],
                            lhsT=wc[:, a, P * t : P * t + P].bitcast(FP8X4),
                            lhsT_scale=ws[:, a, P * t : P * t + P],
                            rhs=x_codes["q"][0][:, a, D * b : D * b + D].bitcast(FP8X4),
                            rhs_scale=x_codes["q"][1][:, a, D * b : D * b + D],
                            start=(a == 0),
                            stop=(a == 1),
                        )
                q_banks[g].append(bank)

        def q_bias(g):
            qg = codp.tile([P, B, D, 4], BF16, tag="qg", name="qg", align_bytes=64, bufs=2)
            for b in range(B):
                nc.vector.tensor_tensor(
                    out=qg[:, b, :, :].rearrange("p (c i) t -> p c t i", i=4),
                    in0=q_banks[g][b][:].rearrange("p t (c i) -> p c t i", i=4),
                    in1=bq_f[:, 4 * g : 4 * g + 4].unsqueeze(1).unsqueeze(3).to_broadcast([P, D // 4, 4, 4]),
                    op=ALU.add,
                )
            q_grouped[g] = qg

        def q_quantise(g):
            nc.vector.quantize_mx(
                out=qc[:, g, :].bitcast(FP8X4),
                scales=qs[:, g, :],
                in_=q_grouped[g][:].rearrange("p b d t -> p (b d t)"),
            )

        s_q = chain_b("q")
        for n in range(4):
            x_bank("v", n, X_EVAC[n])
        next_load()
        pe_gram("v", 0)
        scale_chunk("q", 0, s_q)
        x_codes["v"] = quantise("vx", const, x_grouped["v"], B * N, "vx")
        for i in range(G + 1):
            if i < G:
                quantise_chunk("q", i)
                if i > 0:
                    pe_gram("v", i)
                s_square("v", i)
                if i == G - 1:
                    chain_mask("v")
            if i >= 1:
                q_bias(i - 1)
            if i + 1 < G:
                scale_chunk("q", i + 1, s_q)
            if i >= 1:
                q_quantise(i - 1)
            if i < G:
                for n in range(4):
                    pe_bank("v", i, n)
                    out_bank("v", i, n)
                    if i == G - 1 and n == 1:
                        chain_sum("v")
                next_load()
                if i == G - 1:
                    s_v = chain_b("v")
                    scale_chunk("v", 0, s_v)
                    bv_f = widen("bv_f", late["bv"])
                    hm_f = widen("hm_f", late["hm"])
                    quantise_chunk("v", 0)
                    scale_chunk("v", 1, s_v)
                q_project(i)

        v_sb = const.tile([P, G, 4, B * N], F32, name="v_sb")

        def v_project(g):
            wc, ws = codes[("v", g)]
            for t in range(4):
                bank = ps_t.tile([P, B * N], F32, tag="tp", name="vbank")
                for a in range(2):
                    nc.tensor.matmul_mx(
                        out=bank[:],
                        lhsT=wc[:, a, P * t : P * t + P].bitcast(FP8X4),
                        lhsT_scale=ws[:, a, P * t : P * t + P],
                        rhs=x_codes["v"][0][:, a, :].bitcast(FP8X4),
                        rhs_scale=x_codes["v"][1][:, a, :],
                        start=(a == 0),
                        stop=(a == 1),
                    )
                nc.scalar.activation(
                    out=v_sb[:, g, t, :], in_=bank[:], func=ACT.Identity, bias=bv_f[:, 4 * g + t : 4 * g + t + 1], scale=1.0
                )

        head_codes = {}
        pair_tiles = {}
        planar = {}
        lg_tiles = {}

        def s_mult(h, g):
            if g in VPATH[h]:
                return
            hp = natp.tile([P, 4, B * N], BF16, tag="nat", name="hp")
            for t in range(4):
                nc.scalar.activation(
                    out=hp[:, t, :], in_=v_sb[:, g, t, :], func=ACT.Copy, scale=hm_f[:, 4 * (G * h + g) + t : 4 * (G * h + g) + t + 1]
                )
            planar[(h, g)] = hp

        def v_group(h, g):
            gp, j = g // 2, g % 2
            if g == 0:
                hc_t = hcp.tile([P, G, B * N], U32, tag="hc", name="hc_t", align_bytes=64)
                hs_t = hcp.tile([P, G, B * N], U8, tag="hs", name="hs_t", align_bytes=64)
                head_codes[h] = (hc_t, hs_t)
            if j == 0:
                pair_tiles[(h, gp)] = grpp.tile([P, 2, B * N, 4], BF16, tag="grp", name="hg_t", align_bytes=64)
            hg = pair_tiles[(h, gp)]
            if g in VPATH[h]:
                nc.vector.tensor_tensor(
                    out=hg[:, j, :, :].rearrange("p (c i) t -> p c t i", i=4),
                    in0=v_sb[:, g, :, :].rearrange("p t (c i) -> p c t i", i=4),
                    in1=hm_f[:, 4 * (G * h + g) : 4 * (G * h + g) + 4]
                    .unsqueeze(1)
                    .unsqueeze(3)
                    .to_broadcast([P, B * N // 4, 4, 4]),
                    op=ALU.mult,
                )
            else:
                nc.vector.tensor_copy(
                    out=hg[:, j, :, :].rearrange("p (c i) t -> p c t i", i=4),
                    in_=planar[(h, g)][:].rearrange("p t (c i) -> p c t i", i=4),
                )

        def hv_quantise(h, gp):
            hc, hs = head_codes[h]
            nc.vector.quantize_mx(
                out=hc[:, 2 * gp : 2 * gp + 2, :].rearrange("p g n -> p (g n)").bitcast(FP8X4),
                scales=hs[:, 2 * gp : 2 * gp + 2, :].rearrange("p g n -> p (g n)"),
                in_=pair_tiles[(h, gp)][:].rearrange("p j n t -> p (j n t)"),
            )

        def logits(h):
            hc, hs = head_codes[h]
            lg = ps_m.tile([P, 4, D], F32, tag="misc", name="lg")
            for br in range(4):
                b = br // 2
                for g in range(G):
                    nc.tensor.matmul_mx(
                        out=lg[:, br, :],
                        lhsT=hc[:, g, P * br : P * br + P].bitcast(FP8X4),
                        lhsT_scale=hs[:, g, P * br : P * br + P],
                        rhs=qc[:, g, D * b : D * b + D].bitcast(FP8X4),
                        rhs_scale=qs[:, g, D * b : D * b + D],
                        start=(g == 0),
                        stop=(g == G - 1),
                    )
            lg_tiles[h] = lg

        last_banks = []

        def last_logits(gp):
            hc, hs = head_codes[H - 1]
            if gp == 0:
                for br in range(4):
                    pool, tag = (ps_t, "tp") if br < 3 else (ps_a, "acc")
                    last_banks.append(pool.tile([P, D], F32, tag=tag, name="lg_last"))
            for br in range(4):
                b = br // 2
                for g in (2 * gp, 2 * gp + 1):
                    nc.tensor.matmul_mx(
                        out=last_banks[br][:],
                        lhsT=hc[:, g, P * br : P * br + P].bitcast(FP8X4),
                        lhsT_scale=hs[:, g, P * br : P * br + P],
                        rhs=qc[:, g, D * b : D * b + D].bitcast(FP8X4),
                        rhs_scale=qs[:, g, D * b : D * b + D],
                        start=(g == 0),
                        stop=(g == G - 1),
                    )

        def last_store():
            h = H - 1
            for b in range(B):
                o_sb = outp.tile([P, 2, D], F32, tag="o", name="o_last")
                for r in range(2):
                    if b == 0:
                        nc.scalar.activation(
                            out=o_sb[:, r, :], in_=last_banks[r][:], func=ACT.Identity, bias=hb[:, h : h + 1], scale=1.0
                        )
                    else:
                        nc.vector.tensor_scalar(
                            out=o_sb[:, r, :], in0=last_banks[2 + r][:], scalar1=hb[:, h : h + 1], scalar2=None, op0=ALU.add
                        )
                nc.sync.dma_start(
                    out=out[b, h].rearrange("(m r) d -> m (r d)", r=2), in_=o_sb[:].rearrange("p r d -> p (r d)")
                )

        def store(h):
            o_sb = outp.tile([P, 4, D], F32, tag="o", name="o_sb")
            nc.scalar.activation(out=o_sb[:], in_=lg_tiles[h][:], func=ACT.Identity, bias=hb[:, h : h + 1], scale=1.0)
            nc.sync.dma_start(
                out=out[:, h].rearrange("b (m r) d -> m b (r d)", r=2),
                in_=o_sb[:].rearrange("p (b r) d -> p b (r d)", b=2),
            )

        units = [(h, g) for h in range(H) for g in range(G)]
        U = len(units)
        for i in range(U + S_AHEAD + 1):
            if 1 <= i and i + 1 < G:
                scale_chunk("v", i + 1, s_v)
            if i < G:
                if i >= 1:
                    quantise_chunk("v", i)
                v_project(i)
            if i < U:
                s_mult(units[i][0], units[i][1])
                if units[i][1] == EVAC_LAG and units[i][0] >= 1:
                    store(units[i][0] - 1)
            k = i - S_AHEAD
            if 0 <= k < U:
                v_group(units[k][0], units[k][1])
            if 0 <= k - 1 < U and units[k - 1][1] % 2 == 1:
                hv_quantise(units[k - 1][0], units[k - 1][1] // 2)
                if units[k - 1][0] == H - 1:
                    last_logits(units[k - 1][1] // 2)
                elif units[k - 1][1] == G - 1:
                    logits(units[k - 1][0])
        last_store()
